import numpy as np
import ml_dtypes


def mxq(x, axis, fmt="e4m3"):
    dtype, down = {"e4m3": (ml_dtypes.float8_e4m3fn, 7), "e5m2": (ml_dtypes.float8_e5m2, 14)}[fmt]
    v = np.moveaxis(np.asarray(x, np.float32).astype(ml_dtypes.bfloat16).astype(np.float64), axis, -1)
    blocks = v.reshape(v.shape[:-1] + (-1, 32))
    amax = np.abs(blocks).max(-1, keepdims=True)
    byte = np.maximum(np.where(amax > 0, np.frexp(amax)[1] - 1 + 127, 0) - down, 1)
    scale = np.exp2(byte - 127.0)
    codes = (blocks / scale).astype(np.float32).astype(dtype).astype(np.float64)
    return np.moveaxis((codes * scale).reshape(v.shape), -1, axis)


WIDE = False


def mx_kscale(k):
    if not WIDE:
        return np.ones(k)
    levels = np.array([10, -10, 5, -5, 0])
    if k % 512:
        return np.exp2(np.random.permutation(np.resize(levels, k // 32))).repeat(32)
    a = np.empty((k // 512, 16))
    for p in range(k // 512):
        a[p, :8] = np.random.permutation(np.resize(levels, 8))
        for g in range(8):
            far = levels[np.abs(levels - a[p, g]) >= 10]
            a[p, g + 8] = far[np.random.randint(len(far))]
    return np.exp2(a.ravel()).repeat(32)


BF16 = ml_dtypes.bfloat16


def bf(x):
    return np.asarray(x, np.float32).astype(BF16)


def f64(x):
    return np.asarray(x).astype(np.float64)


N, D, H = 1024, 1024, 2
DH = D // H


def draw0():
    s = np.tile(mx_kscale(DH), H)[:, None]
    t = mx_kscale(N)[None, :]
    return {"q": bf(np.random.standard_normal((D, N)) * 0.15 * s),
            "k": bf(np.random.standard_normal((D, N)) * 0.15 / s * t),
            "v": bf(np.random.standard_normal((D, N)) * 0.15 / t)}


def head(qh, kh, vh):
    sc = mxq(qh.T, 1, "e4m3") @ mxq(kh, 0, "e4m3")
    return mxq(sc, 1, "e4m3") @ mxq(vh.T, 0, "e4m3")


def core(q, k, v):
    q, k, v = f64(q), f64(k), f64(v)
    return np.concatenate([head(q[h * DH:(h + 1) * DH], k[h * DH:(h + 1) * DH], v[h * DH:(h + 1) * DH]) for h in range(H)], axis=1)


def e4m3fn_bytes(y):
    return np.clip(np.asarray(y, np.float64), -448.0, 448.0).astype(np.float32).astype(ml_dtypes.float8_e4m3fn).view(np.uint8)


def e4m3fn_values(b):
    return np.asarray(b, np.uint8).view(ml_dtypes.float8_e4m3fn).astype(np.float64)


def setup_inputs():
    d = draw0()
    x0 = np.asarray(d['v']).astype(np.float64)
    s = (np.max(np.abs(x0), axis=(0,), keepdims=True) / 448.0).astype(np.float32)
    out = {}
    for k, v in d.items():
        if k == 'v':
            out['v_bytes'] = e4m3fn_bytes(x0 / s.astype(np.float64))
            out['v_scale'] = s
        else:
            out[k] = v
    return out


def reference(q, k, v_bytes, v_scale):
    return core(q, k, e4m3fn_values(v_bytes) * v_scale.astype(np.float64))

@@ -1,0 +1,256 @@
+from contextlib import ExitStack
+
+import concourse.mybir as mybir
+from concourse.masks import make_identity
+
+FLOPS = 2 * 2 * 2 * 1024 * 1024 * 512
+
+F32 = mybir.dt.float32
+BF16 = mybir.dt.bfloat16
+U32 = mybir.dt.uint32
+U8 = mybir.dt.uint8
+FP8 = mybir.dt.float8_e4m3fn
+FP8X4 = mybir.dt.float8_e4m3fn_x4
+MULT = mybir.AluOpType.mult
+
+P = 128
+N = 1024
+LOOKAHEAD = 3
+
+
+def tile_mha_pa_kernel(tc, q, k, v_bytes, v_scale, out):
+    nc = tc.nc
+    with ExitStack() as ctx:
+        keep = ctx.enter_context(tc.tile_pool(name="keep", bufs=1))
+        ring = ctx.enter_context(tc.tile_pool(name="ring", bufs=8))
+        many = ctx.enter_context(tc.tile_pool(name="many", bufs=16))
+        psum = ctx.enter_context(tc.psum_pool(name="psum", bufs=8))
+
+        def kt(shape, dt, nm):
+            t = keep.tile(shape, dt, name=nm, align_bytes=64)
+            return t
+
+        HG = [(h, g) for h in range(2) for g in range(2)]
+        k_raw = {hg: kt([P, 4, 512], BF16, "kraw%d%d" % hg) for hg in HG}
+        q_raw = {hg: kt([P, 4, 512], BF16, "qraw%d%d" % hg) for hg in HG}
+        v_raw = {h: kt([P, 4, N], U8, "vraw%d" % h) for h in range(2)}
+        s_bc = kt([P, N], F32, "sbc")
+        k_grp = {hg: kt([P, 512, 4], BF16, "kgrp%d%d" % hg) for hg in HG}
+        q_grp = {hg: kt([P, 512, 4], BF16, "qgrp%d%d" % hg) for hg in HG}
+        v_wide = {(h, r): kt([P, N], BF16, "vwide%d%d" % (h, r)) for h in range(2) for r in range(4)}
+        v_grp = {hg: kt([P, 512, 2], F32, "vgrp%d%d" % hg) for hg in HG}
+        codes = {}
+        scales = {}
+        for nm in "kqv":
+            for hg in HG:
+                codes[(nm,) + hg] = kt([P, 512], U32, "%sc%d%d" % ((nm,) + hg))
+                scales[(nm,) + hg] = kt([P, 512], U8, "%ss%d%d" % ((nm,) + hg))
+        ident = kt([P, P], F32, "ident")
+        dummy = kt([P, 2], F32, "dummy")
+
+        def load_qk(dst, src, h, g, lo, hi):
+            rows = src[512 * h : 512 * (h + 1), :].rearrange("(p j) w -> p j w", j=4)
+            nc.sync.dma_start(out=dst[(h, g)][:, :, lo:hi], in_=rows[:, :, 512 * g + lo : 512 * g + hi])
+
+        def load_v(h):
+            nc.sync.dma_start(
+                out=v_raw[h][:], in_=v_bytes[512 * h : 512 * (h + 1), :].rearrange("(r p) i -> p r i", p=P)
+            )
+
+        load_qk(k_raw, k, 0, 0, 0, 256)
+        load_qk(k_raw, k, 0, 0, 256, 512)
+        load_qk(q_raw, q, 0, 0, 0, 512)
+        load_qk(k_raw, k, 0, 1, 0, 512)
+        load_qk(q_raw, q, 0, 1, 0, 512)
+        nc.sync.dma_start(out=s_bc[:], in_=v_scale.rearrange("o k -> (o k)").partition_broadcast(P))
+        load_v(0)
+        load_qk(k_raw, k, 1, 0, 0, 512)
+        load_qk(q_raw, q, 1, 0, 0, 512)
+        load_v(1)
+        load_qk(k_raw, k, 1, 1, 0, 512)
+        load_qk(q_raw, q, 1, 1, 0, 512)
+
+        nc.gpsimd.memset(dummy[:], 0.0)
+        nc.scalar.copy(out=dummy[:, 1:2], in_=dummy[:, 0:1])
+        make_identity(nc, ident[:])
+
+        def copy(eng, dst, src):
+            if eng == "V":
+                nc.vector.tensor_copy(out=dst, in_=src)
+            else:
+                nc.scalar.copy(out=dst, in_=src)
+
+        def IK(eng, h, g, c):
+            dst = k_grp[(h, g)][:].rearrange("p (t m) j -> p t m j", t=4)[:, :, 64 * c : 64 * (c + 1), :]
+            src = k_raw[(h, g)][:, :, 256 * c : 256 * (c + 1)].rearrange("p j (m t) -> p t m j", t=4)
+            copy(eng, dst, src)
+
+        def IQ(eng, h, c):
+            g, o = c // 2, (c % 2) * 256
+            dst = q_grp[(h, g)][:, o : o + 256, :].rearrange("p (c i) t -> p c t i", i=4)
+            src = q_raw[(h, g)][:, :, o : o + 256].rearrange("p t (c i) -> p c t i", i=4)
+            copy(eng, dst, src)
+
+        def quant(nm, h, g, lo, hi):
+            grp = {"k": k_grp, "q": q_grp}.get(nm)
+            if nm == "v":
+                src = v_grp[(h, g)][:].rearrange("p d u -> p (d u)").bitcast(BF16)
+            else:
+                src = grp[(h, g)][:, lo:hi, :].rearrange("p n j -> p (n j)")
+            nc.vector.quantize_mx(
+                out=codes[(nm, h, g)][:, lo:hi].bitcast(FP8X4), scales=scales[(nm, h, g)][:, lo:hi], in_=src
+            )
+
+        def QK(h, g):
+            quant("k", h, g, 0, 512)
+            made.add(("k", h, g))
+
+        def QQ(h, c):
+            o = (c % 2) * 256
+            quant("q", h, c // 2, o, o + 256)
+            made.add(("q", h, c))
+
+        def QV(h, g):
+            quant("v", h, g, 0, 512)
+            made.add(("v", h, g))
+
+        def MV(h, r):
+            nc.vector.tensor_tensor(out=v_wide[(h, r)][:], in0=v_raw[h][:, r, :].bitcast(FP8), in1=s_bc[:], op=MULT)
+            made.add(("w", h, r))
+
+        made = set()
+        sc_grp = {}
+        sc_codes = {}
+        banks = {}
+
+        def QS(h, jc):
+            c = many.tile([P, 2, 128], U32, name="sccodes", align_bytes=64)
+            s = many.tile([P, 2, 128], U8, name="scscales", align_bytes=64)
+            sc_codes[(h, jc)] = (c, s)
+            made.add(("s", h, jc))
+            nc.vector.quantize_mx(
+                out=c[:].rearrange("p g n -> p (g n)").bitcast(FP8X4),
+                scales=s[:].rearrange("p g n -> p (g n)"),
+                in_=sc_grp[(h, jc)][:].rearrange("p g n t -> p (g n t)"),
+            )
+
+        def fill(d):
+            if d[0] == "E1":
+                h, jc, g = d[1:]
+                b = psum.tile([P, 4, 128], F32, name="bank")
+                ql = 128 * (jc % 4)
+                for t in range(4):
+                    nc.tensor.matmul_mx(
+                        out=b[:, t, :],
+                        lhsT=codes[("k", h, g)][:, 128 * t : 128 * (t + 1)].bitcast(FP8X4),
+                        lhsT_scale=scales[("k", h, g)][:, 128 * t : 128 * (t + 1)],
+                        rhs=codes[("q", h, jc // 4)][:, ql : ql + 128].bitcast(FP8X4),
+                        rhs_scale=scales[("q", h, jc // 4)][:, ql : ql + 128],
+                        start=True,
+                        stop=True,
+                    )
+            elif d[0] == "EV":
+                h, rr, g = d[1:]
+                b = psum.tile([P, 2, 256], F32, name="bank")
+                for r2 in range(2):
+                    words = v_wide[(h, 2 * rr + r2)][:].bitcast(F32)
+                    for u in range(2):
+                        nc.tensor.transpose(
+                            b[:, u, 128 * r2 : 128 * (r2 + 1)], words[:, 256 * g + u : 256 * (g + 1) : 2], ident[:]
+                        )
+            else:
+                h, jc = d[1:]
+                b = psum.tile([P, 512], F32, name="bank")
+                c, s = sc_codes[(h, jc)]
+                for g in range(2):
+                    nc.tensor.matmul_mx(
+                        out=b[:],
+                        lhsT=c[:, g, :].bitcast(FP8X4),
+                        lhsT_scale=s[:, g, :],
+                        rhs=codes[("v", h, g)][:].bitcast(FP8X4),
+                        rhs_scale=scales[("v", h, g)][:],
+                        start=(g == 0),
+                        stop=(g == 1),
+                    )
+            banks[d] = b
+
+        def drain(eng, d):
+            b = banks[d]
+            if d[0] == "E1":
+                h, jc, g = d[1:]
+                if g == 0:
+                    t = ring.tile([P, 2, 128, 4], BF16, name="scgrp", align_bytes=64)
+                    sc_grp[(h, jc)] = t
+                copy(eng, sc_grp[(h, jc)][:, g, :, :], b[:].rearrange("p t n -> p n t"))
+            elif d[0] == "EV":
+                h, rr, g = d[1:]
+                copy(eng, v_grp[(h, g)][:, 256 * rr : 256 * (rr + 1), :], b[:].rearrange("p u d -> p d u"))
+            else:
+                h, jc = d[1:]
+                o = ring.tile([P, 512], F32, name="osb")
+                copy(eng, o[:], b[:])
+                nc.sync.dma_start(out=out[128 * jc : 128 * (jc + 1), 512 * h : 512 * (h + 1)], in_=o[:])
+
+        prog = []
+
+        def w(fn, *a):
+            prog.append(("w", fn, a))
+
+        def e(eng, *d):
+            prog.append(("d", eng, d))
+
+        w(IK, "V", 0, 0, 0), w(IK, "V", 0, 0, 1), w(IQ, "S", 0, 0), w(QK, 0, 0), w(IQ, "V", 0, 1)
+        w(QQ, 0, 0), w(IK, "V", 0, 1, 0), w(IK, "S", 0, 1, 1), w(QQ, 0, 1), w(IQ, "V", 0, 2), w(IQ, "S", 0, 3)
+        w(QK, 0, 1), w(QQ, 0, 2)
+        w(QQ, 0, 3)
+        for jc in range(4):
+            e("S", "E1", 0, jc, 0), w(MV, 0, jc), e("S", "E1", 0, jc, 1)
+            if jc > 0:
+                w(QS, 0, jc - 1)
+        w(QS, 0, 3)
+        w(IQ, "V", 1, 0), w(IK, "V", 1, 0, 0)
+        e("S", "EV", 0, 0, 0), e("S", "E1", 0, 4, 0), e("S", "E1", 0, 4, 1), e("S", "EV", 0, 0, 1), e("S", "EV", 0, 1, 0)
+        w(QS, 0, 4), w(IK, "V", 1, 0, 1), w(QQ, 1, 0)
+        e("S", "E1", 0, 5, 0), e("S", "EV", 0, 1, 1), e("S", "E1", 0, 5, 1)
+        w(QV, 0, 0), w(QV, 0, 1), w(QK, 1, 0), w(QS, 0, 5)
+        e("S", "E1", 0, 6, 0), e("S", "E1", 0, 6, 1), w(IQ, "V", 1, 1), w(QS, 0, 6), w(IK, "V", 1, 1, 0)
+        e("S", "E1", 0, 7, 0), e("S", "E1", 0, 7, 1), w(QQ, 1, 1), w(QS, 0, 7), w(IK, "V", 1, 1, 1)
+        e("S", "E2", 0, 0), e("S", "E2", 0, 1), w(MV, 1, 0), w(QK, 1, 1)
+        e("S", "E2", 0, 2), e("S", "E2", 0, 3), w(MV, 1, 1)
+        e("S", "E2", 0, 4), e("S", "E2", 0, 5), w(MV, 1, 2)
+        e("S", "E1", 1, 0, 0), e("S", "E2", 0, 6), w(MV, 1, 3), w(IQ, "V", 1, 2)
+        e("S", "E1", 1, 0, 1), e("S", "E2", 0, 7), w(QS, 1, 0), w(QQ, 1, 2)
+        e("S", "EV", 1, 0, 0), e("S", "EV", 1, 0, 1), w(IQ, "V", 1, 3)
+        e("S", "E1", 1, 1, 0), e("S", "EV", 1, 1, 0), e("S", "EV", 1, 1, 1), w(QQ, 1, 3), w(QV, 1, 0)
+        e("S", "E1", 1, 1, 1), e("S", "E1", 1, 2, 0), w(QV, 1, 1), w(QS, 1, 1)
+        e("S", "E1", 1, 2, 1), e("V", "E1", 1, 3, 0), e("S", "E1", 1, 3, 1), w(QS, 1, 2), e("V", "E1", 1, 4, 0)
+        e("S", "E2", 1, 0), w(QS, 1, 3)
+        e("S", "E1", 1, 4, 1), e("V", "E1", 1, 5, 0), e("S", "E2", 1, 1), w(QS, 1, 4)
+        e("S", "E1", 1, 5, 1), e("V", "E1", 1, 6, 0), e("S", "E2", 1, 2), w(QS, 1, 5)
+        e("S", "E1", 1, 6, 1), e("V", "E1", 1, 7, 0), e("S", "E2", 1, 3), w(QS, 1, 6)
+        e("S", "E1", 1, 7, 1), e("V", "E2", 1, 4), w(QS, 1, 7)
+        e("S", "E2", 1, 5), e("V", "E2", 1, 6), e("S", "E2", 1, 7)
+
+        drains = [x for x in prog if x[0] == "d"]
+        with tc.manual_schedule():
+            filled = 0
+            seen = 0
+            for item in prog:
+                if item[0] == "w":
+                    item[1](*item[2])
+                else:
+                    while filled < len(drains) and filled <= seen + LOOKAHEAD and ready(drains[filled][2], made):
+                        fill(drains[filled][2])
+                        filled += 1
+                    drain(item[1], item[2])
+                    seen += 1
+
+
+def ready(d, made):
+    if d[0] == "E1":
+        need = [("k", d[1], d[3]), ("q", d[1], d[2] // 2)]
+    elif d[0] == "EV":
+        need = [("w", d[1], 2 * d[2]), ("w", d[1], 2 * d[2] + 1)]
+    else:
+        need = [("s", d[1], d[2]), ("v", d[1], 0), ("v", d[1], 1)]
+    return all(x in made for x in need)

@@ -12,10 +12,33 @@ U8 = mybir.dt.uint8
 FP8 = mybir.dt.float8_e4m3fn
 FP8X4 = mybir.dt.float8_e4m3fn_x4
 MULT = mybir.AluOpType.mult
+ADD = mybir.AluOpType.add
 
 P = 128
 N = 1024
-LOOKAHEAD = 3
+HEADS = 2
+HALF = 512
+
+LOOKAHEAD = 4
+
+K_PIECES = {"k00": (0, 0, 512), "k01": (0, 512, 1024), "k10": (1, 0, 1024)}
+Q_PIECES = {"q0c0": (0, 0, 256), "q00": (0, 256, 1024), "q10": (1, 0, 1024)}
+LOADS = "v00 v01 v02 s v03 k00 q0c0 k01 q00 k10 v1 q10"
+
+ORDER = """
+    V CS01, S CS00, G IQ00, S CS03, V CS02, V EV001, V EV000, S IK000+,
+    V EV011, V QK00, V IK011, V EV010, S IK010, V QK01, V IK110, G IQ02,
+    S IQ01, V QQ00+, S IQ03, S IK111, V CS12+, S CS10+, S IQ13, G IQ12,
+    V QQ02+, V E1021, S E1020, S E1010, S E1011, V EV111, V EV100, V EV110,
+    V EV101, G IQ10, G IQ11, S E1030, S E1041, S E1070, S E1040, S E1051,
+    S E1061, V E1000, V QK11, V IK100+, S E1031, V QQ12+, S E1050, V QK10,
+    S E1060, V QQ10+, S E1071, V QS04+, S E1001, S E1151, S E1150, S E1120,
+    V QV00+, V E1141, S E1101, S E1140, V QS06+, S E1110, V QS00+, V QS02+,
+    S E1100, V E1131, S E204, V E205, S E1130, S E1111, S E206, V QS14+,
+    V QS10+, S E207, S E203, V QV10+, S E200, V E1121, V E1161, S E201,
+    S E202, V QS12+, V E1160, V E1170, S E211, S E215, S E210, S E214,
+    S E212, V QS16, V E1171, S E213, S E216, V QS17, S E3171, S E3170
+"""
 
 
 def tile_mha_pa_kernel(tc, q, k, v_bytes, v_scale, out):
@@ -23,52 +46,49 @@ def tile_mha_pa_kernel(tc, q, k, v_bytes, v_scale, out):
     with ExitStack() as ctx:
         keep = ctx.enter_context(tc.tile_pool(name="keep", bufs=1))
         ring = ctx.enter_context(tc.tile_pool(name="ring", bufs=8))
-        many = ctx.enter_context(tc.tile_pool(name="many", bufs=16))
+        pairs = ctx.enter_context(tc.tile_pool(name="pairs", bufs=8))
         psum = ctx.enter_context(tc.psum_pool(name="psum", bufs=8))
 
-        def kt(shape, dt, nm):
-            t = keep.tile(shape, dt, name=nm, align_bytes=64)
+        def kept(shape, dt, name):
+            t = keep.tile(shape, dt, name=name, align_bytes=64)
             return t
 
-        HG = [(h, g) for h in range(2) for g in range(2)]
-        k_raw = {hg: kt([P, 4, 512], BF16, "kraw%d%d" % hg) for hg in HG}
-        q_raw = {hg: kt([P, 4, 512], BF16, "qraw%d%d" % hg) for hg in HG}
-        v_raw = {h: kt([P, 4, N], U8, "vraw%d" % h) for h in range(2)}
-        s_bc = kt([P, N], F32, "sbc")
-        k_grp = {hg: kt([P, 512, 4], BF16, "kgrp%d%d" % hg) for hg in HG}
-        q_grp = {hg: kt([P, 512, 4], BF16, "qgrp%d%d" % hg) for hg in HG}
-        v_wide = {(h, r): kt([P, N], BF16, "vwide%d%d" % (h, r)) for h in range(2) for r in range(4)}
-        v_grp = {hg: kt([P, 512, 2], F32, "vgrp%d%d" % hg) for hg in HG}
-        codes = {}
-        scales = {}
-        for nm in "kqv":
-            for hg in HG:
-                codes[(nm,) + hg] = kt([P, 512], U32, "%sc%d%d" % ((nm,) + hg))
-                scales[(nm,) + hg] = kt([P, 512], U8, "%ss%d%d" % ((nm,) + hg))
-        ident = kt([P, P], F32, "ident")
-        dummy = kt([P, 2], F32, "dummy")
+        k_raw = {x: kept([P, 4, x[2] - x[1]], BF16, "kraw%d_%d" % x[:2]) for x in [K_PIECES[name] for name in K_PIECES]}
+        q_raw = {x: kept([P, 4, x[2] - x[1]], BF16, "qraw%d_%d" % x[:2]) for x in [Q_PIECES[name] for name in Q_PIECES]}
+        v0_raw = [kept([P, N], U8, "v0raw%d" % r) for r in range(4)]
+        v1_raw = kept([P, 4, N], U8, "v1raw")
+        scale_col = kept([P, 2, 4], F32, "scalecol")
 
-        def load_qk(dst, src, h, g, lo, hi):
-            rows = src[512 * h : 512 * (h + 1), :].rearrange("(p j) w -> p j w", j=4)
-            nc.sync.dma_start(out=dst[(h, g)][:, :, lo:hi], in_=rows[:, :, 512 * g + lo : 512 * g + hi])
+        HG = [(h, g) for h in range(HEADS) for g in range(2)]
+        k_grp = {hg: kept([P, HALF, 4], BF16, "kgrp%d%d" % hg) for hg in HG}
+        q_grp = {hg: kept([P, HALF, 4], BF16, "qgrp%d%d" % hg) for hg in HG}
+        k_codes = {hg: kept([P, HALF], U32, "kcodes%d%d" % hg) for hg in HG}
+        k_scales = {hg: kept([P, HALF], U8, "kscales%d%d" % hg) for hg in HG}
+        q_codes = {hg: kept([P, HALF], U32, "qcodes%d%d" % hg) for hg in HG}
+        q_scales = {hg: kept([P, HALF], U8, "qscales%d%d" % hg) for hg in HG}
+        v_wide = [kept([P, 4, N], BF16, "vwide%d" % h) for h in range(HEADS)]
+        v_grp = [kept([P, 2, HALF, 4], BF16, "vgrp%d" % h) for h in range(HEADS)]
+        v_codes = [kept([P, 2, HALF], U32, "vcodes%d" % h) for h in range(HEADS)]
+        v_scales = [kept([P, 2, HALF], U8, "vscales%d" % h) for h in range(HEADS)]
+        ident = kept([P, P], F32, "ident")
+        dummy = kept([P, 2], F32, "dummy")
 
-        def load_v(h):
-            nc.sync.dma_start(
-                out=v_raw[h][:], in_=v_bytes[512 * h : 512 * (h + 1), :].rearrange("(r p) i -> p r i", p=P)
-            )
+        def load(name):
+            if name == "s":
+                nc.sync.dma_start(out=scale_col[:], in_=v_scale.rearrange("o (g p t) -> p (o g) t", p=P, t=4))
+            elif name == "v1":
+                nc.sync.dma_start(out=v1_raw[:], in_=v_bytes[HALF:N, :].rearrange("(r p) i -> p r i", p=P))
+            elif name[0] == "v":
+                r = int(name[2])
+                nc.sync.dma_start(out=v0_raw[r][:], in_=v_bytes[P * r : P * (r + 1), :])
+            else:
+                raw, src, piece = (k_raw, k, K_PIECES[name]) if name[0] == "k" else (q_raw, q, Q_PIECES[name])
+                h, lo, hi = piece
+                rows = src[HALF * h : HALF * (h + 1), :].rearrange("(p t) w -> p t w", t=4)
+                nc.sync.dma_start(out=raw[piece][:], in_=rows[:, :, lo:hi])
 
-        load_qk(k_raw, k, 0, 0, 0, 256)
-        load_qk(k_raw, k, 0, 0, 256, 512)
-        load_qk(q_raw, q, 0, 0, 0, 512)
-        load_qk(k_raw, k, 0, 1, 0, 512)
-        load_qk(q_raw, q, 0, 1, 0, 512)
-        nc.sync.dma_start(out=s_bc[:], in_=v_scale.rearrange("o k -> (o k)").partition_broadcast(P))
-        load_v(0)
-        load_qk(k_raw, k, 1, 0, 0, 512)
-        load_qk(q_raw, q, 1, 0, 0, 512)
-        load_v(1)
-        load_qk(k_raw, k, 1, 1, 0, 512)
-        load_qk(q_raw, q, 1, 1, 0, 512)
+        for name in LOADS.split(" "):
+            load(name)
 
         nc.gpsimd.memset(dummy[:], 0.0)
         nc.scalar.copy(out=dummy[:, 1:2], in_=dummy[:, 0:1])
@@ -77,180 +97,184 @@ def tile_mha_pa_kernel(tc, q, k, v_bytes, v_scale, out):
         def copy(eng, dst, src):
             if eng == "V":
                 nc.vector.tensor_copy(out=dst, in_=src)
-            else:
+            elif eng == "S":
                 nc.scalar.copy(out=dst, in_=src)
-
-        def IK(eng, h, g, c):
-            dst = k_grp[(h, g)][:].rearrange("p (t m) j -> p t m j", t=4)[:, :, 64 * c : 64 * (c + 1), :]
-            src = k_raw[(h, g)][:, :, 256 * c : 256 * (c + 1)].rearrange("p j (m t) -> p t m j", t=4)
-            copy(eng, dst, src)
-
-        def IQ(eng, h, c):
-            g, o = c // 2, (c % 2) * 256
-            dst = q_grp[(h, g)][:, o : o + 256, :].rearrange("p (c i) t -> p c t i", i=4)
-            src = q_raw[(h, g)][:, :, o : o + 256].rearrange("p t (c i) -> p c t i", i=4)
-            copy(eng, dst, src)
-
-        def quant(nm, h, g, lo, hi):
-            grp = {"k": k_grp, "q": q_grp}.get(nm)
-            if nm == "v":
-                src = v_grp[(h, g)][:].rearrange("p d u -> p (d u)").bitcast(BF16)
             else:
-                src = grp[(h, g)][:, lo:hi, :].rearrange("p n j -> p (n j)")
-            nc.vector.quantize_mx(
-                out=codes[(nm, h, g)][:, lo:hi].bitcast(FP8X4), scales=scales[(nm, h, g)][:, lo:hi], in_=src
-            )
+                nc.gpsimd.tensor_scalar(out=dst, in0=src, scalar1=1.0, scalar2=0.0, op0=MULT, op1=ADD)
 
-        def QK(h, g):
-            quant("k", h, g, 0, 512)
-            made.add(("k", h, g))
-
-        def QQ(h, c):
-            o = (c % 2) * 256
-            quant("q", h, c // 2, o, o + 256)
-            made.add(("q", h, c))
-
-        def QV(h, g):
-            quant("v", h, g, 0, 512)
-            made.add(("v", h, g))
-
-        def MV(h, r):
-            nc.vector.tensor_tensor(out=v_wide[(h, r)][:], in0=v_raw[h][:, r, :].bitcast(FP8), in1=s_bc[:], op=MULT)
-            made.add(("w", h, r))
+        def tokens(raw, h, lo, hi):
+            for x in raw:
+                if x[0] == h and x[1] <= lo and hi <= x[2]:
+                    return raw[x][:, :, lo - x[1] : hi - x[1]]
 
         made = set()
+
+        def IK(eng, n, h, g, c):
+            lo, hi = 2 * c, 2 * (c + n)
+            dst = k_grp[(h, g)][:, P * lo : P * hi, :].rearrange("p (s m) t -> p m t s", m=P)
+            src = tokens(k_raw, h, HALF * g, HALF * (g + 1)).rearrange("p t (m s) -> p m t s", s=4)
+            copy(eng, dst, src[:, :, :, lo:hi])
+
+        def IQ(eng, n, h, c):
+            o = (c % 2) * 256
+            dst = q_grp[(h, c // 2)][:, o : o + 256 * n, :]
+            src = tokens(q_raw, h, 256 * c, 256 * (c + n))
+            if eng == "G":
+                copy(eng, dst, src.rearrange("p t w -> p w t"))
+            else:
+                copy(eng, dst.rearrange("p (c i) t -> p c t i", i=4), src.rearrange("p t (c i) -> p c t i", i=4))
+
+        def quantise(codes, scales, grp):
+            nc.vector.quantize_mx(out=codes.bitcast(FP8X4), scales=scales, in_=grp)
+
+        def QK(eng, n, h, g):
+            quantise(k_codes[(h, g)][:], k_scales[(h, g)][:], k_grp[(h, g)][:].rearrange("p w t -> p (w t)"))
+            made.add(("k", h, g))
+
+        def QQ(eng, n, h, c):
+            hg, lo, hi = (h, c // 2), (c % 2) * 256, (c % 2 + n) * 256
+            src = q_grp[hg][:, lo:hi, :].rearrange("p w t -> p (w t)")
+            quantise(q_codes[hg][:, lo:hi], q_scales[hg][:, lo:hi], src)
+            for x in range(c, c + n):
+                made.add(("q", h, x))
+
+        def CS(eng, n, h, r):
+            if h == 0:
+                copy(eng, v_wide[0][:, r, :], v0_raw[r][:].bitcast(FP8))
+            else:
+                copy(eng, v_wide[1][:, r : r + n, :], v1_raw[:, r : r + n, :].bitcast(FP8))
+            for x in range(r, r + n):
+                made.add(("w", h, x))
+
+        def QV(eng, n, h, g):
+            quantise(
+                v_codes[h][:, g : g + n, :].rearrange("p g d -> p (g d)"),
+                v_scales[h][:, g : g + n, :].rearrange("p g d -> p (g d)"),
+                v_grp[h][:, g : g + n, :, :].rearrange("p g d t -> p (g d t)"),
+            )
+            for x in range(g, g + n):
+                made.add(("v", h, x))
+
         sc_grp = {}
         sc_codes = {}
+
+        def QS(eng, n, h, j):
+            pair, u = (h, j // 2), j % 2
+            if pair not in sc_codes:
+                codes = pairs.tile([P, 2, 2, P], U32, name="sccodes", align_bytes=64)
+                scales = pairs.tile([P, 2, 2, P], U8, name="scscales", align_bytes=64)
+                sc_codes[pair] = (codes, scales)
+            codes, scales = sc_codes[pair]
+            quantise(
+                codes[:, u : u + n].rearrange("p u g w -> p (u g w)"),
+                scales[:, u : u + n].rearrange("p u g w -> p (u g w)"),
+                sc_grp[pair][:, u : u + n].rearrange("p u g w t -> p (u g w t)"),
+            )
+            for x in range(j, j + n):
+                made.add(("s", h, x))
+
         banks = {}
 
-        def QS(h, jc):
-            c = many.tile([P, 2, 128], U32, name="sccodes", align_bytes=64)
-            s = many.tile([P, 2, 128], U8, name="scscales", align_bytes=64)
-            sc_codes[(h, jc)] = (c, s)
-            made.add(("s", h, jc))
-            nc.vector.quantize_mx(
-                out=c[:].rearrange("p g n -> p (g n)").bitcast(FP8X4),
-                scales=s[:].rearrange("p g n -> p (g n)"),
-                in_=sc_grp[(h, jc)][:].rearrange("p g n t -> p (g n t)"),
+        def fill_E1(h, j, g):
+            bank = psum.tile([P, 4, P], F32, name="bank")
+            cols = slice(P * (j % 4), P * (j % 4) + P)
+            for s in range(4):
+                nc.tensor.matmul_mx(
+                    out=bank[:, s, :],
+                    lhsT=k_codes[(h, g)][:, P * s : P * (s + 1)].bitcast(FP8X4),
+                    lhsT_scale=k_scales[(h, g)][:, P * s : P * (s + 1)],
+                    rhs=q_codes[(h, j // 4)][:, cols].bitcast(FP8X4),
+                    rhs_scale=q_scales[(h, j // 4)][:, cols],
+                    start=True,
+                    stop=True,
+                )
+            return bank
+
+        def E1(eng, n, h, j, g):
+            pair = (h, j // 2)
+            if pair not in sc_grp:
+                grp = pairs.tile([P, 2, 2, P, 4], BF16, name="scgrp", align_bytes=64)
+                sc_grp[pair] = grp
+            copy(eng, sc_grp[pair][:, j % 2, g, :, :], banks[("E1", h, j, g)][:].rearrange("p s w -> p w s"))
+
+        def fill_EV(h, r, g):
+            bank = psum.tile([P, 2, 256], F32, name="bank")
+            for x in range(2):
+                words = v_wide[h][:, 2 * r + x, :].bitcast(F32)
+                for u in range(2):
+                    nc.tensor.transpose(
+                        bank[:, u, P * x : P * (x + 1)], words[:, 256 * g + u : 256 * (g + 1) : 2], ident[:]
+                    )
+            return bank
+
+        def EV(eng, n, h, r, g):
+            nc.vector.tensor_tensor(
+                out=v_grp[h][:, g, 256 * r : 256 * (r + 1), :].rearrange("p d (u e) -> p d u e", u=2),
+                in0=banks[("EV", h, r, g)][:].bitcast(BF16).rearrange("p u (d e) -> p d u e", e=2),
+                in1=scale_col[:, g : g + 1, :].to_broadcast([P, 256, 4]).rearrange("p d (u e) -> p d u e", u=2),
+                op=MULT,
             )
 
-        def fill(d):
-            if d[0] == "E1":
-                h, jc, g = d[1:]
-                b = psum.tile([P, 4, 128], F32, name="bank")
-                ql = 128 * (jc % 4)
-                for t in range(4):
-                    nc.tensor.matmul_mx(
-                        out=b[:, t, :],
-                        lhsT=codes[("k", h, g)][:, 128 * t : 128 * (t + 1)].bitcast(FP8X4),
-                        lhsT_scale=scales[("k", h, g)][:, 128 * t : 128 * (t + 1)],
-                        rhs=codes[("q", h, jc // 4)][:, ql : ql + 128].bitcast(FP8X4),
-                        rhs_scale=scales[("q", h, jc // 4)][:, ql : ql + 128],
-                        start=True,
-                        stop=True,
-                    )
-            elif d[0] == "EV":
-                h, rr, g = d[1:]
-                b = psum.tile([P, 2, 256], F32, name="bank")
-                for r2 in range(2):
-                    words = v_wide[(h, 2 * rr + r2)][:].bitcast(F32)
-                    for u in range(2):
-                        nc.tensor.transpose(
-                            b[:, u, 128 * r2 : 128 * (r2 + 1)], words[:, 256 * g + u : 256 * (g + 1) : 2], ident[:]
-                        )
-            else:
-                h, jc = d[1:]
-                b = psum.tile([P, 512], F32, name="bank")
-                c, s = sc_codes[(h, jc)]
-                for g in range(2):
-                    nc.tensor.matmul_mx(
-                        out=b[:],
-                        lhsT=c[:, g, :].bitcast(FP8X4),
-                        lhsT_scale=s[:, g, :],
-                        rhs=codes[("v", h, g)][:].bitcast(FP8X4),
-                        rhs_scale=scales[("v", h, g)][:],
-                        start=(g == 0),
-                        stop=(g == 1),
-                    )
-            banks[d] = b
+        def fill_out(h, j, lo, hi):
+            bank = psum.tile([P, hi - lo], F32, name="bank")
+            codes, scales = sc_codes[(h, j // 2)]
+            for g in range(2):
+                nc.tensor.matmul_mx(
+                    out=bank[:],
+                    lhsT=codes[:, j % 2, g, :].bitcast(FP8X4),
+                    lhsT_scale=scales[:, j % 2, g, :],
+                    rhs=v_codes[h][:, g, lo:hi].bitcast(FP8X4),
+                    rhs_scale=v_scales[h][:, g, lo:hi],
+                    start=(g == 0),
+                    stop=(g == 1),
+                )
+            return bank
 
-        def drain(eng, d):
-            b = banks[d]
-            if d[0] == "E1":
-                h, jc, g = d[1:]
-                if g == 0:
-                    t = ring.tile([P, 2, 128, 4], BF16, name="scgrp", align_bytes=64)
-                    sc_grp[(h, jc)] = t
-                copy(eng, sc_grp[(h, jc)][:, g, :, :], b[:].rearrange("p t n -> p n t"))
-            elif d[0] == "EV":
-                h, rr, g = d[1:]
-                copy(eng, v_grp[(h, g)][:, 256 * rr : 256 * (rr + 1), :], b[:].rearrange("p u d -> p d u"))
-            else:
-                h, jc = d[1:]
-                o = ring.tile([P, 512], F32, name="osb")
-                copy(eng, o[:], b[:])
-                nc.sync.dma_start(out=out[128 * jc : 128 * (jc + 1), 512 * h : 512 * (h + 1)], in_=o[:])
+        def store(eng, bank, h, j, lo, hi):
+            o = ring.tile([P, hi - lo], F32, name="osb")
+            copy(eng, o[:], bank[:])
+            nc.sync.dma_start(out=out[P * j : P * (j + 1), HALF * h + lo : HALF * h + hi], in_=o[:])
 
-        prog = []
+        def fill_E2(h, j):
+            return fill_out(h, j, 0, HALF)
 
-        def w(fn, *a):
-            prog.append(("w", fn, a))
+        def E2(eng, n, h, j):
+            store(eng, banks[("E2", h, j)], h, j, 0, HALF)
 
-        def e(eng, *d):
-            prog.append(("d", eng, d))
+        def fill_E3(h, j, a):
+            return fill_out(h, j, 256 * a, 256 * (a + 1))
 
-        w(IK, "V", 0, 0, 0), w(IK, "V", 0, 0, 1), w(IQ, "S", 0, 0), w(QK, 0, 0), w(IQ, "V", 0, 1)
-        w(QQ, 0, 0), w(IK, "V", 0, 1, 0), w(IK, "S", 0, 1, 1), w(QQ, 0, 1), w(IQ, "V", 0, 2), w(IQ, "S", 0, 3)
-        w(QK, 0, 1), w(QQ, 0, 2)
-        w(QQ, 0, 3)
-        for jc in range(4):
-            e("S", "E1", 0, jc, 0), w(MV, 0, jc), e("S", "E1", 0, jc, 1)
-            if jc > 0:
-                w(QS, 0, jc - 1)
-        w(QS, 0, 3)
-        w(IQ, "V", 1, 0), w(IK, "V", 1, 0, 0)
-        e("S", "EV", 0, 0, 0), e("S", "E1", 0, 4, 0), e("S", "E1", 0, 4, 1), e("S", "EV", 0, 0, 1), e("S", "EV", 0, 1, 0)
-        w(QS, 0, 4), w(IK, "V", 1, 0, 1), w(QQ, 1, 0)
-        e("S", "E1", 0, 5, 0), e("S", "EV", 0, 1, 1), e("S", "E1", 0, 5, 1)
-        w(QV, 0, 0), w(QV, 0, 1), w(QK, 1, 0), w(QS, 0, 5)
-        e("S", "E1", 0, 6, 0), e("S", "E1", 0, 6, 1), w(IQ, "V", 1, 1), w(QS, 0, 6), w(IK, "V", 1, 1, 0)
-        e("S", "E1", 0, 7, 0), e("S", "E1", 0, 7, 1), w(QQ, 1, 1), w(QS, 0, 7), w(IK, "V", 1, 1, 1)
-        e("S", "E2", 0, 0), e("S", "E2", 0, 1), w(MV, 1, 0), w(QK, 1, 1)
-        e("S", "E2", 0, 2), e("S", "E2", 0, 3), w(MV, 1, 1)
-        e("S", "E2", 0, 4), e("S", "E2", 0, 5), w(MV, 1, 2)
-        e("S", "E1", 1, 0, 0), e("S", "E2", 0, 6), w(MV, 1, 3), w(IQ, "V", 1, 2)
-        e("S", "E1", 1, 0, 1), e("S", "E2", 0, 7), w(QS, 1, 0), w(QQ, 1, 2)
-        e("S", "EV", 1, 0, 0), e("S", "EV", 1, 0, 1), w(IQ, "V", 1, 3)
-        e("S", "E1", 1, 1, 0), e("S", "EV", 1, 1, 0), e("S", "EV", 1, 1, 1), w(QQ, 1, 3), w(QV, 1, 0)
-        e("S", "E1", 1, 1, 1), e("S", "E1", 1, 2, 0), w(QV, 1, 1), w(QS, 1, 1)
-        e("S", "E1", 1, 2, 1), e("V", "E1", 1, 3, 0), e("S", "E1", 1, 3, 1), w(QS, 1, 2), e("V", "E1", 1, 4, 0)
-        e("S", "E2", 1, 0), w(QS, 1, 3)
-        e("S", "E1", 1, 4, 1), e("V", "E1", 1, 5, 0), e("S", "E2", 1, 1), w(QS, 1, 4)
-        e("S", "E1", 1, 5, 1), e("V", "E1", 1, 6, 0), e("S", "E2", 1, 2), w(QS, 1, 5)
-        e("S", "E1", 1, 6, 1), e("V", "E1", 1, 7, 0), e("S", "E2", 1, 3), w(QS, 1, 6)
-        e("S", "E1", 1, 7, 1), e("V", "E2", 1, 4), w(QS, 1, 7)
-        e("S", "E2", 1, 5), e("V", "E2", 1, 6), e("S", "E2", 1, 7)
+        def E3(eng, n, h, j, a):
+            store(eng, banks[("E3", h, j, a)], h, j, 256 * a, 256 * (a + 1))
 
-        drains = [x for x in prog if x[0] == "d"]
+        fills = {"E1": fill_E1, "EV": fill_EV, "E2": fill_E2, "E3": fill_E3}
+        needs = {
+            "E1": lambda h, j, g: [("k", h, g), ("q", h, j // 2)],
+            "EV": lambda h, r, g: [("w", h, 2 * r), ("w", h, 2 * r + 1)],
+            "E2": lambda h, j: [("s", h, j), ("v", h, 0), ("v", h, 1)],
+            "E3": lambda h, j, a: [("s", h, j), ("v", h, 0), ("v", h, 1)],
+        }
+        step_fns = {
+            "IK": IK, "IQ": IQ, "QK": QK, "QQ": QQ, "CS": CS, "QV": QV, "QS": QS, "E1": E1, "EV": EV, "E2": E2, "E3": E3
+        }
+
+        steps = []
+        for word in ORDER.split(","):
+            eng, name = word.split()
+            n = 2 if name[-1] == "+" else 1
+            steps.append((eng, n, name[:2], tuple(int(x) for x in name[2:].replace("+", ""))))
+        fillable = [(kind,) + at for eng, n, kind, at in steps if kind in fills]
+
         with tc.manual_schedule():
             filled = 0
-            seen = 0
-            for item in prog:
-                if item[0] == "w":
-                    item[1](*item[2])
-                else:
-                    while filled < len(drains) and filled <= seen + LOOKAHEAD and ready(drains[filled][2], made):
-                        fill(drains[filled][2])
+            emptied = 0
+            for eng, n, kind, at in steps:
+                if kind in fills:
+                    while filled < len(fillable) and filled <= emptied + LOOKAHEAD:
+                        b = fillable[filled]
+                        if not all(x in made for x in needs[b[0]](*b[1:])):
+                            break
+                        banks[b] = fills[b[0]](*b[1:])
                         filled += 1
-                    drain(item[1], item[2])
-                    seen += 1
-
-
-def ready(d, made):
-    if d[0] == "E1":
-        need = [("k", d[1], d[3]), ("q", d[1], d[2] // 2)]
-    elif d[0] == "EV":
-        need = [("w", d[1], 2 * d[2]), ("w", d[1], 2 * d[2] + 1)]
-    else:
-        need = [("s", d[1], d[2]), ("v", d[1], 0), ("v", d[1], 1)]
-    return all(x in made for x in need)
+                    emptied += 1
+                step_fns[kind](eng, n, *at)

from contextlib import ExitStack

import concourse.mybir as mybir
from concourse.masks import make_identity

FLOPS = 2 * 2 * 2 * 1024 * 1024 * 512

F32 = mybir.dt.float32
BF16 = mybir.dt.bfloat16
U32 = mybir.dt.uint32
U8 = mybir.dt.uint8
FP8 = mybir.dt.float8_e4m3fn
FP8X4 = mybir.dt.float8_e4m3fn_x4
MULT = mybir.AluOpType.mult
ADD = mybir.AluOpType.add

P = 128
N = 1024
HEADS = 2
HALF = 512

LOOKAHEAD = 4

K_PIECES = {"k00": (0, 0, 512), "k01": (0, 512, 1024), "k10": (1, 0, 1024)}
Q_PIECES = {"q0c0": (0, 0, 256), "q00": (0, 256, 1024), "q10": (1, 0, 1024)}
LOADS = "v00 v01 v02 s v03 k00 q0c0 k01 q00 k10 v1 q10"

ORDER = """
    V CS01, S CS00, G IQ00, S CS03, V CS02, V EV001, V EV000, S IK000+,
    V EV011, V QK00, V IK011, V EV010, S IK010, V QK01, V IK110, G IQ02,
    S IQ01, V QQ00+, S IQ03, S IK111, V CS12+, S CS10+, S IQ13, G IQ12,
    V QQ02+, V E1021, S E1020, S E1010, S E1011, V EV111, V EV100, V EV110,
    V EV101, G IQ10, G IQ11, S E1030, S E1041, S E1070, S E1040, S E1051,
    S E1061, V E1000, V QK11, V IK100+, S E1031, V QQ12+, S E1050, V QK10,
    S E1060, V QQ10+, S E1071, V QS04+, S E1001, S E1151, S E1150, S E1120,
    V QV00+, V E1141, S E1101, S E1140, V QS06+, S E1110, V QS00+, V QS02+,
    S E1100, V E1131, S E204, V E205, S E1130, S E1111, S E206, V QS14+,
    V QS10+, S E207, S E203, V QV10+, S E200, V E1121, V E1161, S E201,
    S E202, V QS12+, V E1160, V E1170, S E211, S E215, S E210, S E214,
    S E212, V QS16, V E1171, S E213, S E216, V QS17, S E3171, S E3170
"""


def tile_mha_pa_kernel(tc, q, k, v_bytes, v_scale, out):
    nc = tc.nc
    with ExitStack() as ctx:
        keep = ctx.enter_context(tc.tile_pool(name="keep", bufs=1))
        ring = ctx.enter_context(tc.tile_pool(name="ring", bufs=8))
        pairs = ctx.enter_context(tc.tile_pool(name="pairs", bufs=8))
        psum = ctx.enter_context(tc.psum_pool(name="psum", bufs=8))

        def kept(shape, dt, name):
            t = keep.tile(shape, dt, name=name, align_bytes=64)
            return t

        k_raw = {x: kept([P, 4, x[2] - x[1]], BF16, "kraw%d_%d" % x[:2]) for x in [K_PIECES[name] for name in K_PIECES]}
        q_raw = {x: kept([P, 4, x[2] - x[1]], BF16, "qraw%d_%d" % x[:2]) for x in [Q_PIECES[name] for name in Q_PIECES]}
        v0_raw = [kept([P, N], U8, "v0raw%d" % r) for r in range(4)]
        v1_raw = kept([P, 4, N], U8, "v1raw")
        scale_col = kept([P, 2, 4], F32, "scalecol")

        HG = [(h, g) for h in range(HEADS) for g in range(2)]
        k_grp = {hg: kept([P, HALF, 4], BF16, "kgrp%d%d" % hg) for hg in HG}
        q_grp = {hg: kept([P, HALF, 4], BF16, "qgrp%d%d" % hg) for hg in HG}
        k_codes = {hg: kept([P, HALF], U32, "kcodes%d%d" % hg) for hg in HG}
        k_scales = {hg: kept([P, HALF], U8, "kscales%d%d" % hg) for hg in HG}
        q_codes = {hg: kept([P, HALF], U32, "qcodes%d%d" % hg) for hg in HG}
        q_scales = {hg: kept([P, HALF], U8, "qscales%d%d" % hg) for hg in HG}
        v_wide = [kept([P, 4, N], BF16, "vwide%d" % h) for h in range(HEADS)]
        v_grp = [kept([P, 2, HALF, 4], BF16, "vgrp%d" % h) for h in range(HEADS)]
        v_codes = [kept([P, 2, HALF], U32, "vcodes%d" % h) for h in range(HEADS)]
        v_scales = [kept([P, 2, HALF], U8, "vscales%d" % h) for h in range(HEADS)]
        ident = kept([P, P], F32, "ident")
        dummy = kept([P, 2], F32, "dummy")

        def load(name):
            if name == "s":
                nc.sync.dma_start(out=scale_col[:], in_=v_scale.rearrange("o (g p t) -> p (o g) t", p=P, t=4))
            elif name == "v1":
                nc.sync.dma_start(out=v1_raw[:], in_=v_bytes[HALF:N, :].rearrange("(r p) i -> p r i", p=P))
            elif name[0] == "v":
                r = int(name[2])
                nc.sync.dma_start(out=v0_raw[r][:], in_=v_bytes[P * r : P * (r + 1), :])
            else:
                raw, src, piece = (k_raw, k, K_PIECES[name]) if name[0] == "k" else (q_raw, q, Q_PIECES[name])
                h, lo, hi = piece
                rows = src[HALF * h : HALF * (h + 1), :].rearrange("(p t) w -> p t w", t=4)
                nc.sync.dma_start(out=raw[piece][:], in_=rows[:, :, lo:hi])

        for name in LOADS.split(" "):
            load(name)

        nc.gpsimd.memset(dummy[:], 0.0)
        nc.scalar.copy(out=dummy[:, 1:2], in_=dummy[:, 0:1])
        make_identity(nc, ident[:])

        def copy(eng, dst, src):
            if eng == "V":
                nc.vector.tensor_copy(out=dst, in_=src)
            elif eng == "S":
                nc.scalar.copy(out=dst, in_=src)
            else:
                nc.gpsimd.tensor_scalar(out=dst, in0=src, scalar1=1.0, scalar2=0.0, op0=MULT, op1=ADD)

        def tokens(raw, h, lo, hi):
            for x in raw:
                if x[0] == h and x[1] <= lo and hi <= x[2]:
                    return raw[x][:, :, lo - x[1] : hi - x[1]]

        made = set()

        def IK(eng, n, h, g, c):
            lo, hi = 2 * c, 2 * (c + n)
            dst = k_grp[(h, g)][:, P * lo : P * hi, :].rearrange("p (s m) t -> p m t s", m=P)
            src = tokens(k_raw, h, HALF * g, HALF * (g + 1)).rearrange("p t (m s) -> p m t s", s=4)
            copy(eng, dst, src[:, :, :, lo:hi])

        def IQ(eng, n, h, c):
            o = (c % 2) * 256
            dst = q_grp[(h, c // 2)][:, o : o + 256 * n, :]
            src = tokens(q_raw, h, 256 * c, 256 * (c + n))
            if eng == "G":
                copy(eng, dst, src.rearrange("p t w -> p w t"))
            else:
                copy(eng, dst.rearrange("p (c i) t -> p c t i", i=4), src.rearrange("p t (c i) -> p c t i", i=4))

        def quantise(codes, scales, grp):
            nc.vector.quantize_mx(out=codes.bitcast(FP8X4), scales=scales, in_=grp)

        def QK(eng, n, h, g):
            quantise(k_codes[(h, g)][:], k_scales[(h, g)][:], k_grp[(h, g)][:].rearrange("p w t -> p (w t)"))
            made.add(("k", h, g))

        def QQ(eng, n, h, c):
            hg, lo, hi = (h, c // 2), (c % 2) * 256, (c % 2 + n) * 256
            src = q_grp[hg][:, lo:hi, :].rearrange("p w t -> p (w t)")
            quantise(q_codes[hg][:, lo:hi], q_scales[hg][:, lo:hi], src)
            for x in range(c, c + n):
                made.add(("q", h, x))

        def CS(eng, n, h, r):
            if h == 0:
                copy(eng, v_wide[0][:, r, :], v0_raw[r][:].bitcast(FP8))
            else:
                copy(eng, v_wide[1][:, r : r + n, :], v1_raw[:, r : r + n, :].bitcast(FP8))
            for x in range(r, r + n):
                made.add(("w", h, x))

        def QV(eng, n, h, g):
            quantise(
                v_codes[h][:, g : g + n, :].rearrange("p g d -> p (g d)"),
                v_scales[h][:, g : g + n, :].rearrange("p g d -> p (g d)"),
                v_grp[h][:, g : g + n, :, :].rearrange("p g d t -> p (g d t)"),
            )
            for x in range(g, g + n):
                made.add(("v", h, x))

        sc_grp = {}
        sc_codes = {}

        def QS(eng, n, h, j):
            pair, u = (h, j // 2), j % 2
            if pair not in sc_codes:
                codes = pairs.tile([P, 2, 2, P], U32, name="sccodes", align_bytes=64)
                scales = pairs.tile([P, 2, 2, P], U8, name="scscales", align_bytes=64)
                sc_codes[pair] = (codes, scales)
            codes, scales = sc_codes[pair]
            quantise(
                codes[:, u : u + n].rearrange("p u g w -> p (u g w)"),
                scales[:, u : u + n].rearrange("p u g w -> p (u g w)"),
                sc_grp[pair][:, u : u + n].rearrange("p u g w t -> p (u g w t)"),
            )
            for x in range(j, j + n):
                made.add(("s", h, x))

        banks = {}

        def fill_E1(h, j, g):
            bank = psum.tile([P, 4, P], F32, name="bank")
            cols = slice(P * (j % 4), P * (j % 4) + P)
            for s in range(4):
                nc.tensor.matmul_mx(
                    out=bank[:, s, :],
                    lhsT=k_codes[(h, g)][:, P * s : P * (s + 1)].bitcast(FP8X4),
                    lhsT_scale=k_scales[(h, g)][:, P * s : P * (s + 1)],
                    rhs=q_codes[(h, j // 4)][:, cols].bitcast(FP8X4),
                    rhs_scale=q_scales[(h, j // 4)][:, cols],
                    start=True,
                    stop=True,
                )
            return bank

        def E1(eng, n, h, j, g):
            pair = (h, j // 2)
            if pair not in sc_grp:
                grp = pairs.tile([P, 2, 2, P, 4], BF16, name="scgrp", align_bytes=64)
                sc_grp[pair] = grp
            copy(eng, sc_grp[pair][:, j % 2, g, :, :], banks[("E1", h, j, g)][:].rearrange("p s w -> p w s"))

        def fill_EV(h, r, g):
            bank = psum.tile([P, 2, 256], F32, name="bank")
            for x in range(2):
                words = v_wide[h][:, 2 * r + x, :].bitcast(F32)
                for u in range(2):
                    nc.tensor.transpose(
                        bank[:, u, P * x : P * (x + 1)], words[:, 256 * g + u : 256 * (g + 1) : 2], ident[:]
                    )
            return bank

        def EV(eng, n, h, r, g):
            nc.vector.tensor_tensor(
                out=v_grp[h][:, g, 256 * r : 256 * (r + 1), :].rearrange("p d (u e) -> p d u e", u=2),
                in0=banks[("EV", h, r, g)][:].bitcast(BF16).rearrange("p u (d e) -> p d u e", e=2),
                in1=scale_col[:, g : g + 1, :].to_broadcast([P, 256, 4]).rearrange("p d (u e) -> p d u e", u=2),
                op=MULT,
            )

        def fill_out(h, j, lo, hi):
            bank = psum.tile([P, hi - lo], F32, name="bank")
            codes, scales = sc_codes[(h, j // 2)]
            for g in range(2):
                nc.tensor.matmul_mx(
                    out=bank[:],
                    lhsT=codes[:, j % 2, g, :].bitcast(FP8X4),
                    lhsT_scale=scales[:, j % 2, g, :],
                    rhs=v_codes[h][:, g, lo:hi].bitcast(FP8X4),
                    rhs_scale=v_scales[h][:, g, lo:hi],
                    start=(g == 0),
                    stop=(g == 1),
                )
            return bank

        def store(eng, bank, h, j, lo, hi):
            o = ring.tile([P, hi - lo], F32, name="osb")
            copy(eng, o[:], bank[:])
            nc.sync.dma_start(out=out[P * j : P * (j + 1), HALF * h + lo : HALF * h + hi], in_=o[:])

        def fill_E2(h, j):
            return fill_out(h, j, 0, HALF)

        def E2(eng, n, h, j):
            store(eng, banks[("E2", h, j)], h, j, 0, HALF)

        def fill_E3(h, j, a):
            return fill_out(h, j, 256 * a, 256 * (a + 1))

        def E3(eng, n, h, j, a):
            store(eng, banks[("E3", h, j, a)], h, j, 256 * a, 256 * (a + 1))

        fills = {"E1": fill_E1, "EV": fill_EV, "E2": fill_E2, "E3": fill_E3}
        needs = {
            "E1": lambda h, j, g: [("k", h, g), ("q", h, j // 2)],
            "EV": lambda h, r, g: [("w", h, 2 * r), ("w", h, 2 * r + 1)],
            "E2": lambda h, j: [("s", h, j), ("v", h, 0), ("v", h, 1)],
            "E3": lambda h, j, a: [("s", h, j), ("v", h, 0), ("v", h, 1)],
        }
        step_fns = {
            "IK": IK, "IQ": IQ, "QK": QK, "QQ": QQ, "CS": CS, "QV": QV, "QS": QS, "E1": E1, "EV": EV, "E2": E2, "E3": E3
        }

        steps = []
        for word in ORDER.split(","):
            eng, name = word.split()
            n = 2 if name[-1] == "+" else 1
            steps.append((eng, n, name[:2], tuple(int(x) for x in name[2:].replace("+", ""))))
        fillable = [(kind,) + at for eng, n, kind, at in steps if kind in fills]

        with tc.manual_schedule():
            filled = 0
            emptied = 0
            for eng, n, kind, at in steps:
                if kind in fills:
                    while filled < len(fillable) and filled <= emptied + LOOKAHEAD:
                        b = fillable[filled]
                        if not all(x in made for x in needs[b[0]](*b[1:])):
                            break
                        banks[b] = fills[b[0]](*b[1:])
                        filled += 1
                    emptied += 1
                step_fns[kind](eng, n, *at)
